import numpy as np
import ml_dtypes


def mxq(x, axis, fmt="e4m3"):
    dtype, down = {"e4m3": (ml_dtypes.float8_e4m3fn, 7), "e5m2": (ml_dtypes.float8_e5m2, 14)}[fmt]
    v = np.moveaxis(np.asarray(x, np.float32).astype(ml_dtypes.bfloat16).astype(np.float64), axis, -1)
    blocks = v.reshape(v.shape[:-1] + (-1, 32))
    amax = np.abs(blocks).max(-1, keepdims=True)
    byte = np.maximum(np.where(amax > 0, np.frexp(amax)[1] - 1 + 127, 0) - down, 1)
    scale = np.exp2(byte - 127.0)
    codes = (blocks / scale).astype(np.float32).astype(dtype).astype(np.float64)
    return np.moveaxis((codes * scale).reshape(v.shape), -1, axis)


WIDE = False


def mx_kscale(k):
    if not WIDE:
        return np.ones(k)
    levels = np.array([10, -10, 5, -5, 0])
    if k % 512:
        return np.exp2(np.random.permutation(np.resize(levels, k // 32))).repeat(32)
    a = np.empty((k // 512, 16))
    for p in range(k // 512):
        a[p, :8] = np.random.permutation(np.resize(levels, 8))
        for g in range(8):
            far = levels[np.abs(levels - a[p, g]) >= 10]
            a[p, g + 8] = far[np.random.randint(len(far))]
    return np.exp2(a.ravel()).repeat(32)


BF16 = ml_dtypes.bfloat16


def bf(x):
    return np.asarray(x, np.float32).astype(BF16)


def f64(x):
    return np.asarray(x).astype(np.float64)


B, T, C, H, NOPE, ROPE, VD, LORA = 4, 1024, 1024, 2, 128, 512, 128, 512
EPS = 1e-6
HALF = ROPE // 2
KVW = H * (NOPE + VD)


def make_freq_cis():
    inv = 1.0 / (10000.0 ** (np.arange(0, ROPE, 2) / ROPE))
    ang = np.outer(np.arange(T), inv)
    return np.stack([np.cos(ang), np.sin(ang)], -1)


def apply_rope(v, fc):
    vr = v.reshape(B, T, HALF, 2)
    real = vr[..., 0] * fc[..., 0] - vr[..., 1] * fc[..., 1]
    imag = vr[..., 1] * fc[..., 0] + vr[..., 0] * fc[..., 1]
    return np.stack([real, imag], -1).reshape(B, T, ROPE)


def setup_inputs():
    s, t = mx_kscale(C), mx_kscale(LORA)
    return {"x": bf(np.random.standard_normal((B, T, C)) * s),
            "freq_cis": bf(make_freq_cis()),
            "Wckv": bf(np.random.standard_normal((C, LORA + ROPE)) / np.sqrt(C) / s[:, None]),
            "kv_norm_w": bf((1.0 + 0.1 * np.random.standard_normal(LORA)) * t),
            "Wdkv": bf(np.random.standard_normal((LORA, KVW)) / np.sqrt(LORA) / t[:, None])}


def reference(x, freq_cis, Wckv, kv_norm_w, Wdkv):
    ckv = mxq(f64(x), 2, "e4m3") @ mxq(f64(Wckv), 0, "e4m3")
    kv_lat, k_rope = ckv[..., :LORA], ckv[..., LORA:]
    k_rope = apply_rope(k_rope, f64(freq_cis))
    lat_n = kv_lat / np.sqrt(np.mean(kv_lat * kv_lat, -1, keepdims=True) + EPS) * f64(kv_norm_w)
    kv = mxq(lat_n, 2, "e4m3") @ mxq(f64(Wdkv), 0, "e4m3")
    return kv, k_rope

@@ -1,0 +1,336 @@
+from contextlib import ExitStack
+
+import concourse.mybir as mybir
+from concourse.masks import make_identity
+
+F32 = mybir.dt.float32
+BF16 = mybir.dt.bfloat16
+U32 = mybir.dt.uint32
+U8 = mybir.dt.uint8
+FP8X4 = mybir.dt.float8_e4m3fn_x4
+ALU = mybir.AluOpType
+ACT = mybir.ActivationFunctionType
+
+B, T, C, LORA, ROPE, KVW = 4, 1024, 1024, 512, 512, 512
+EPS = 1e-6
+P = 128
+PACK = 4
+K_PASS = P * PACK
+PASSES = C // K_PASS
+assert PASSES == 2
+J = T // P
+TILES = B * J
+HALF = ROPE // 2
+X_LEAD = 2
+ROPE_LAG = 1
+LATE_PER_STEP = 2
+
+FLOPS = 2 * B * T * C * (LORA + ROPE) + 2 * B * T * LORA * KVW
+
+
+def regroup(nc, grouped, raw, cols):
+    split = cols * 3 // 4
+    for copy, lo, hi in ((nc.vector.tensor_copy, 0, split), (nc.scalar.copy, split, cols)):
+        copy(
+            out=grouped[:, lo:hi, :].rearrange("p (c i) t -> p c t i", i=4),
+            in_=raw[:, :, lo:hi].rearrange("p t (c i) -> p c t i", i=4),
+        )
+
+
+def regroup_permuted(nc, grouped, raw, cols):
+    split = cols // PACK * 3 // 4
+    for copy, lo, hi in ((nc.vector.tensor_copy, 0, split), (nc.scalar.copy, split, cols // PACK)):
+        copy(
+            out=grouped[:].rearrange("p (s m) t -> p s m t", s=PACK)[:, :, lo:hi, :],
+            in_=raw[:].rearrange("p t (m s) -> p s m t", s=PACK)[:, :, lo:hi, :],
+        )
+
+
+def tile_multiheadlatentattention_pa_t_kernel(
+    tc, x, freq_cis, Wckv, kv_norm_w, Wdkv, out_0, out_1
+):
+    nc = tc.nc
+    x_view = x.rearrange("b (p j) c -> b p j c", j=J)
+    table_view = freq_cis.rearrange("(p j) i two -> p j (i two)", j=J)
+    kv_view = out_0.rearrange("b (p j) f -> b p j f", j=J)
+    rope_view = out_1.rearrange("b (p j) f -> b p j f", j=J)
+
+    with ExitStack() as ctx:
+        keep = ctx.enter_context(tc.tile_pool(name="keep", bufs=1))
+        x_pool = ctx.enter_context(tc.tile_pool(name="x_pool", bufs=TILES))
+        stage = ctx.enter_context(tc.tile_pool(name="stage", bufs=2))
+        work = ctx.enter_context(tc.tile_pool(name="work", bufs=3))
+        small = ctx.enter_context(tc.tile_pool(name="small", bufs=4))
+        outs = ctx.enter_context(tc.tile_pool(name="outs", bufs=6))
+        psum = ctx.enter_context(tc.psum_pool(name="psum", bufs=1))
+        ctx.enter_context(tc.manual_schedule())
+
+        eps = keep.tile([P, 1], F32)
+        nc.vector.memset(eps[:], EPS)
+        warm = keep.tile([P, 1], F32)
+        nc.scalar.activation(out=warm[:], in_=eps[:], func=ACT.Sqrt)
+        ident_f32 = keep.tile([P, P], F32)
+        make_identity(nc, ident_f32[:])
+        ident_bf16 = keep.tile([P, P], BF16)
+        make_identity(nc, ident_bf16[:])
+        ones = keep.tile([P, P], BF16)
+        nc.vector.memset(ones[:], 1.0)
+        gain_rows = keep.tile([P, LORA], BF16)
+        nc.vector.memset(gain_rows[:], 0.0)
+
+        x_tiles = []
+
+        def load_x(count):
+            for i in range(len(x_tiles), len(x_tiles) + count):
+                b, j = divmod(i, J)
+                x_sb = x_pool.tile([P, C], BF16, name="x_sb")
+                nc.sync.dma_start(out=x_sb[:], in_=x_view[b, :, j, :])
+                x_tiles.append(x_sb)
+
+        def load_w_half(n0):
+            raws = []
+            for g in range(PASSES):
+                w_raw = stage.tile([P, PACK, LORA], BF16, name="w_raw", bufs=2 * PASSES + 1)
+                k0 = K_PASS * g
+                nc.sync.dma_start(
+                    out=w_raw[:],
+                    in_=Wckv[k0 : k0 + K_PASS, n0 : n0 + LORA].rearrange("(p t) c -> p t c", t=PACK),
+                )
+                raws.append(w_raw)
+            return raws
+
+        table = keep.tile([P, J, ROPE], BF16)
+        load_x(1)
+        lat_raws = load_w_half(0)
+        nc.sync.dma_start(out=gain_rows[0:1, :], in_=kv_norm_w.unsqueeze(0))
+        load_x(2)
+        rope_raws = load_w_half(LORA)
+        load_x(1)
+        wd_raw = stage.tile([P, PACK, KVW], BF16, name="w_raw", bufs=2 * PASSES + 1)
+        nc.sync.dma_start(out=wd_raw[:], in_=Wdkv.rearrange("(p t) n -> p t n", t=PACK))
+        nc.sync.dma_start(out=table[:, 0 : J // 2, :], in_=table_view[:, 0 : J // 2, :])
+        load_x(2)
+        nc.sync.dma_start(out=table[:, J // 2 : J, :], in_=table_view[:, J // 2 : J, :])
+        load_x(TILES - len(x_tiles))
+
+        w_codes = keep.tile([P, PASSES, LORA + ROPE], U32, align_bytes=64)
+        w_scales = keep.tile([P, PASSES, LORA + ROPE], U8, align_bytes=64)
+        wd_codes = keep.tile([P, KVW], U32, align_bytes=64)
+        wd_scales = keep.tile([P, KVW], U8, align_bytes=64)
+        gain = keep.tile([P, LORA], F32)
+
+        live = {}
+
+        def transpose_x(i):
+            words = x_tiles[i][:].bitcast(F32)
+            xt = psum.tile([P, PASSES, 2, P], F32, tag="xt", bufs=2)
+            for g in range(PASSES):
+                for u in range(2):
+                    w0 = 2 * P * g
+                    nc.tensor.transpose(xt[:, g, u, :], words[:, w0 + u : w0 + 2 * P : 2], ident_f32[:])
+            live["xt", i] = xt
+
+        def group_x(i):
+            xt = live["xt", i]
+            x_grouped = work.tile([P, PASSES * P * PACK], BF16, align_bytes=64)
+            nc.scalar.copy(
+                out=x_grouped[:].bitcast(F32).rearrange("p (g r u) -> p g r u", g=PASSES, u=2),
+                in_=xt[:].rearrange("p g u r -> p g r u"),
+            )
+            live["x_grouped", i] = x_grouped
+
+        def quantise_x(i):
+            x_grouped = live["x_grouped", i]
+            x_codes = work.tile([P, PASSES * P], U32, bufs=X_LEAD + ROPE_LAG + 1, align_bytes=64)
+            x_scales = work.tile([P, PASSES * P], U8, bufs=X_LEAD + ROPE_LAG + 1, align_bytes=64)
+            nc.vector.quantize_mx(out=x_codes[:].bitcast(FP8X4), scales=x_scales[:], in_=x_grouped[:])
+            live["x_mx", i] = (x_codes, x_scales)
+
+        def first_matmul(i, acc, n0):
+            x_codes, x_scales = live["x_mx", i]
+            for g in range(PASSES):
+                tokens = slice(g * P, (g + 1) * P)
+                nc.tensor.matmul_mx(
+                    out=acc[:],
+                    lhsT=x_codes[:, tokens].bitcast(FP8X4),
+                    lhsT_scale=x_scales[:, tokens],
+                    rhs=w_codes[:, g, n0 : n0 + LORA].bitcast(FP8X4),
+                    rhs_scale=w_scales[:, g, n0 : n0 + LORA],
+                    start=(g == 0),
+                    stop=(g == PASSES - 1),
+                )
+
+        def matmul_lat(i):
+            lat = psum.tile([P, LORA], F32, tag="lat", bufs=2)
+            first_matmul(i, lat, 0)
+            live["lat", i] = lat
+
+        def matmul_kr(i):
+            kr = psum.tile([P, ROPE], F32, tag="kr", bufs=2)
+            first_matmul(i, kr, LORA)
+            live["kr", i] = kr
+
+        def sum_squares(i):
+            lat = live["lat", i]
+            squares = work.tile([P, LORA], BF16)
+            sum_sq = small.tile([P, 1], F32)
+            nc.scalar.activation(out=squares[:], in_=lat[:], func=ACT.Square, accum_out=sum_sq[:])
+            live["sum_sq", i] = sum_sq
+
+        def root_mean_square(i):
+            rms = small.tile([P, 1], F32)
+            nc.scalar.activation(
+                out=rms[:], in_=live["sum_sq", i][:], func=ACT.Sqrt, bias=EPS, scale=1.0 / LORA
+            )
+            live["rms", i] = rms
+
+        def invert_rms(i):
+            inv_rms = small.tile([P, 1], F32)
+            nc.vector.reciprocal(out=inv_rms[:], in_=live["rms", i][:])
+            live["inv_rms", i] = inv_rms
+
+        def pairs_of(i):
+            kr = live["kr", i][:].rearrange("p (i e) -> p i e", e=2)
+            cos_sin = table[:, i % J, :].rearrange("p (i two) -> p i two", two=2)
+            return kr, cos_sin
+
+        def rotate_by_cos(i):
+            kr, cos_sin = pairs_of(i)
+            by_cos = work.tile([P, HALF, 2], F32)
+            nc.vector.tensor_tensor(
+                out=by_cos[:], in0=kr, in1=cos_sin[:, :, 0:1].to_broadcast([P, HALF, 2]), op=ALU.mult
+            )
+            live["by_cos", i] = by_cos
+
+        def rotate_by_sin(i):
+            kr, cos_sin = pairs_of(i)
+            by_sin = work.tile([P, 2, HALF], F32)
+            nc.vector.scalar_tensor_tensor(
+                out=by_sin[:, 0, :], in0=kr[:, :, 1], scalar=-1.0, in1=cos_sin[:, :, 1],
+                op0=ALU.mult, op1=ALU.mult,
+            )
+            nc.vector.tensor_tensor(out=by_sin[:, 1, :], in0=kr[:, :, 0], in1=cos_sin[:, :, 1], op=ALU.mult)
+            live["by_sin", i] = by_sin
+
+        def normalise(i):
+            lat = live["lat", i]
+            inv_rms = live["inv_rms", i]
+            n_bf16 = work.tile([P, LORA], BF16)
+            nc.vector.scalar_tensor_tensor(
+                out=n_bf16[:], in0=lat[:], scalar=inv_rms[:], in1=gain[:], op0=ALU.mult, op1=ALU.mult
+            )
+            live["n", i] = n_bf16
+
+        def rotate_sum(i):
+            rope_sb = outs.tile([P, ROPE], F32)
+            nc.gpsimd.tensor_tensor(
+                out=rope_sb[:].rearrange("p (i e) -> p i e", e=2),
+                in0=live["by_cos", i][:],
+                in1=live["by_sin", i][:].rearrange("p e i -> p i e"),
+                op=ALU.add,
+            )
+            nc.sync.dma_start(out=rope_view[i // J, :, i % J, :], in_=rope_sb[:])
+
+        def transpose_n(i):
+            n_bf16 = live["n", i]
+            nt = psum.tile([P, PACK, P], BF16, tag="nt")
+            for t in range(PACK):
+                nc.tensor.transpose(nt[:, t, :], n_bf16[:, t * P : (t + 1) * P], ident_bf16[:])
+            live["nt", i] = nt
+
+        def group_n(i):
+            nt = live["nt", i]
+            n_grouped = work.tile([P, P, PACK], BF16, align_bytes=64)
+            nc.scalar.copy(out=n_grouped[:], in_=nt[:].rearrange("p t r -> p r t"))
+            live["n_grouped", i] = n_grouped
+
+        def quantise_n(i):
+            n_grouped = live["n_grouped", i]
+            n_codes = work.tile([P, P], U32, align_bytes=64)
+            n_scales = work.tile([P, P], U8, align_bytes=64)
+            nc.vector.quantize_mx(
+                out=n_codes[:].bitcast(FP8X4), scales=n_scales[:],
+                in_=n_grouped[:].rearrange("p r t -> p (r t)"),
+            )
+            live["n_mx", i] = (n_codes, n_scales)
+
+        def second_matmul(i):
+            n_codes, n_scales = live["n_mx", i]
+            kv = psum.tile([P, KVW], F32, tag="kv")
+            nc.tensor.matmul_mx(
+                out=kv[:],
+                lhsT=n_codes[:].bitcast(FP8X4), lhsT_scale=n_scales[:],
+                rhs=wd_codes[:].bitcast(FP8X4), rhs_scale=wd_scales[:],
+                start=True, stop=True,
+            )
+            live["kv", i] = kv
+
+        def copy_kv(i):
+            kv_sb = outs.tile([P, KVW], F32)
+            nc.scalar.copy(out=kv_sb[:], in_=live["kv", i][:])
+            nc.sync.dma_start(out=kv_view[i // J, :, i % J, :], in_=kv_sb[:])
+
+        def regroup_piece(piece, regroup_fn=regroup):
+            w_grouped = stage.tile([P, LORA, PACK], BF16, bufs=3, align_bytes=64)
+            regroup_fn(nc, w_grouped, piece[0], LORA)
+            return w_grouped
+
+        def quantise_piece(piece, w_grouped):
+            nc.vector.quantize_mx(
+                out=piece[1].bitcast(FP8X4),
+                scales=piece[2],
+                in_=w_grouped[:].rearrange("p c t -> p (c t)"),
+            )
+
+        lat_pieces = [(lat_raws[g], w_codes[:, g, 0:LORA], w_scales[:, g, 0:LORA]) for g in range(PASSES)]
+        late_pieces = [
+            (rope_raws[g], w_codes[:, g, LORA : LORA + ROPE], w_scales[:, g, LORA : LORA + ROPE])
+            for g in range(PASSES)
+        ]
+        late_pieces.append((wd_raw, wd_codes[:], wd_scales[:]))
+
+        transpose_x(0)
+        group_x(0)
+        grouped_0 = regroup_piece(lat_pieces[0], regroup_permuted)
+        quantise_x(0)
+        grouped_1 = regroup_piece(lat_pieces[1], regroup_permuted)
+        quantise_piece(lat_pieces[0], grouped_0)
+        quantise_piece(lat_pieces[1], grouped_1)
+        for i in range(1, X_LEAD):
+            transpose_x(i)
+            group_x(i)
+            quantise_x(i)
+
+        gain_ps = psum.tile([P, LORA], F32, tag="kv")
+        nc.tensor.matmul(gain_ps[:], lhsT=ones[:], rhs=gain_rows[:], start=True, stop=True)
+        nc.scalar.copy(
+            out=gain[:].rearrange("p (t m) -> p t m", t=PACK),
+            in_=gain_ps[:].rearrange("p (m t) -> p t m", t=PACK),
+        )
+
+        def run(stage_fn, i):
+            if 0 <= i < TILES:
+                stage_fn(i)
+
+        for s in range(TILES + 3):
+            late_now = late_pieces[LATE_PER_STEP * s : LATE_PER_STEP * (s + 1)]
+            run(transpose_x, s + X_LEAD)
+            run(transpose_n, s - 2)
+            run(group_x, s + X_LEAD)
+            run(group_n, s - 2)
+            late_grouped = [regroup_piece(piece) for piece in late_now]
+            run(matmul_lat, s)
+            run(matmul_kr, s - ROPE_LAG)
+            run(second_matmul, s - 3)
+            run(sum_squares, s)
+            run(copy_kv, s - 3)
+            run(root_mean_square, s)
+            run(invert_rms, s - 1)
+            run(rotate_by_cos, s - ROPE_LAG - 1)
+            run(normalise, s - 1)
+            run(rotate_by_sin, s - ROPE_LAG - 1)
+            run(quantise_x, s + X_LEAD)
+            run(quantise_n, s - 2)
+            for piece, w_grouped in zip(late_now, late_grouped):
+                quantise_piece(piece, w_grouped)
+            run(rotate_sum, s - ROPE_LAG - 1)

@@ -39,11 +39,12 @@ def regroup(nc, grouped, raw, cols):
 
 def regroup_permuted(nc, grouped, raw, cols):
     split = cols // PACK * 3 // 4
-    for copy, lo, hi in ((nc.vector.tensor_copy, 0, split), (nc.scalar.copy, split, cols // PACK)):
-        copy(
-            out=grouped[:].rearrange("p (s m) t -> p s m t", s=PACK)[:, :, lo:hi, :],
-            in_=raw[:].rearrange("p t (m s) -> p s m t", s=PACK)[:, :, lo:hi, :],
-        )
+    for u in range(2):
+        for copy, lo, hi in ((nc.vector.tensor_copy, 0, split), (nc.scalar.copy, split, cols // PACK)):
+            copy(
+                out=grouped[:].rearrange("p (u m e) t -> p u m e t", u=2, e=2)[:, u, lo:hi, :, :],
+                in_=raw[:].rearrange("p t (m u e) -> p u m e t", u=2, e=2)[:, u, lo:hi, :, :],
+            )
 
 
 def tile_multiheadlatentattention_pa_t_kernel(
@@ -71,8 +72,6 @@ def tile_multiheadlatentattention_pa_t_kernel(
         nc.scalar.activation(out=warm[:], in_=eps[:], func=ACT.Sqrt)
         ident_f32 = keep.tile([P, P], F32)
         make_identity(nc, ident_f32[:])
-        ident_bf16 = keep.tile([P, P], BF16)
-        make_identity(nc, ident_bf16[:])
         ones = keep.tile([P, P], BF16)
         nc.vector.memset(ones[:], 1.0)
         gain_rows = keep.tile([P, LORA], BF16)
@@ -232,16 +231,19 @@ def tile_multiheadlatentattention_pa_t_kernel(
             nc.sync.dma_start(out=rope_view[i // J, :, i % J, :], in_=rope_sb[:])
 
         def transpose_n(i):
-            n_bf16 = live["n", i]
-            nt = psum.tile([P, PACK, P], BF16, tag="nt")
-            for t in range(PACK):
-                nc.tensor.transpose(nt[:, t, :], n_bf16[:, t * P : (t + 1) * P], ident_bf16[:])
+            words = live["n", i][:].bitcast(F32)
+            nt = psum.tile([P, 2, P], F32, tag="nt")
+            for u in range(2):
+                nc.tensor.transpose(nt[:, u, :], words[:, u * P : (u + 1) * P], ident_f32[:])
             live["nt", i] = nt
 
         def group_n(i):
             nt = live["nt", i]
             n_grouped = work.tile([P, P, PACK], BF16, align_bytes=64)
-            nc.scalar.copy(out=n_grouped[:], in_=nt[:].rearrange("p t r -> p r t"))
+            nc.scalar.copy(
+                out=n_grouped[:].rearrange("p r t -> p (r t)").bitcast(F32).rearrange("p (r u) -> p r u", u=2),
+                in_=nt[:].rearrange("p u r -> p r u"),
+            )
             live["n_grouped", i] = n_grouped
 
         def quantise_n(i):
@@ -304,18 +306,19 @@ def tile_multiheadlatentattention_pa_t_kernel(
         gain_ps = psum.tile([P, LORA], F32, tag="kv")
         nc.tensor.matmul(gain_ps[:], lhsT=ones[:], rhs=gain_rows[:], start=True, stop=True)
         nc.scalar.copy(
-            out=gain[:].rearrange("p (t m) -> p t m", t=PACK),
-            in_=gain_ps[:].rearrange("p (m t) -> p t m", t=PACK),
+            out=gain[:].rearrange("p (u m e) -> p u m e", u=2, e=2),
+            in_=gain_ps[:].rearrange("p (m u e) -> p u m e", u=2, e=2),
         )
 
         def run(stage_fn, i):
             if 0 <= i < TILES:
                 stage_fn(i)
 
-        for s in range(TILES + 3):
+        for s in range(TILES + 4):
             late_now = late_pieces[LATE_PER_STEP * s : LATE_PER_STEP * (s + 1)]
             run(transpose_x, s + X_LEAD)
             run(transpose_n, s - 2)
+            run(copy_kv, s - 4)
             run(group_x, s + X_LEAD)
             run(group_n, s - 2)
             late_grouped = [regroup_piece(piece) for piece in late_now]
@@ -323,7 +326,6 @@ def tile_multiheadlatentattention_pa_t_kernel(
             run(matmul_kr, s - ROPE_LAG)
             run(second_matmul, s - 3)
             run(sum_squares, s)
-            run(copy_kv, s - 3)
             run(root_mean_square, s)
             run(invert_rms, s - 1)
             run(rotate_by_cos, s - ROPE_LAG - 1)

@@ -69,7 +69,7 @@ def tile_multiheadlatentattention_pa_t_kernel(
         eps = keep.tile([P, 1], F32)
         nc.vector.memset(eps[:], EPS)
         warm = keep.tile([P, 1], F32)
-        nc.scalar.activation(out=warm[:], in_=eps[:], func=ACT.Sqrt)
+        nc.scalar.activation(out=warm[:], in_=eps[:], func=ACT.Abs_reciprocal_sqrt)
         ident_f32 = keep.tile([P, P], F32)
         make_identity(nc, ident_f32[:])
         ones = keep.tile([P, P], BF16)
@@ -176,16 +176,11 @@ def tile_multiheadlatentattention_pa_t_kernel(
             nc.scalar.activation(out=squares[:], in_=lat[:], func=ACT.Square, accum_out=sum_sq[:])
             live["sum_sq", i] = sum_sq
 
-        def root_mean_square(i):
-            rms = small.tile([P, 1], F32)
-            nc.scalar.activation(
-                out=rms[:], in_=live["sum_sq", i][:], func=ACT.Sqrt, bias=EPS, scale=1.0 / LORA
-            )
-            live["rms", i] = rms
-
         def invert_rms(i):
             inv_rms = small.tile([P, 1], F32)
-            nc.vector.reciprocal(out=inv_rms[:], in_=live["rms", i][:])
+            nc.scalar.activation(
+                out=inv_rms[:], in_=live["sum_sq", i][:], func=ACT.Abs_reciprocal_sqrt, bias=EPS, scale=1.0 / LORA
+            )
             live["inv_rms", i] = inv_rms
 
         def pairs_of(i):
@@ -326,8 +321,7 @@ def tile_multiheadlatentattention_pa_t_kernel(
             run(matmul_kr, s - ROPE_LAG)
             run(second_matmul, s - 3)
             run(sum_squares, s)
-            run(root_mean_square, s)
-            run(invert_rms, s - 1)
+            run(invert_rms, s)
             run(rotate_by_cos, s - ROPE_LAG - 1)
             run(normalise, s - 1)
             run(rotate_by_sin, s - ROPE_LAG - 1)

@@ -24,6 +24,7 @@ HALF = ROPE // 2
 X_LEAD = 2
 ROPE_LAG = 1
 LATE_PER_STEP = 2
+SHORT_BANKS = 4
 
 FLOPS = 2 * B * T * C * (LORA + ROPE) + 2 * B * T * LORA * KVW
 
@@ -122,7 +123,7 @@ def tile_multiheadlatentattention_pa_t_kernel(
 
         def transpose_x(i):
             words = x_tiles[i][:].bitcast(F32)
-            xt = psum.tile([P, PASSES, 2, P], F32, tag="xt", bufs=2)
+            xt = psum.tile([P, PASSES, 2, P], F32, tag="short", bufs=SHORT_BANKS)
             for g in range(PASSES):
                 for u in range(2):
                     w0 = 2 * P * g
@@ -227,7 +228,7 @@ def tile_multiheadlatentattention_pa_t_kernel(
 
         def transpose_n(i):
             words = live["n", i][:].bitcast(F32)
-            nt = psum.tile([P, 2, P], F32, tag="nt")
+            nt = psum.tile([P, 2, P], F32, tag="short", bufs=SHORT_BANKS)
             for u in range(2):
                 nc.tensor.transpose(nt[:, u, :], words[:, u * P : (u + 1) * P], ident_f32[:])
             live["nt", i] = nt
@@ -253,7 +254,7 @@ def tile_multiheadlatentattention_pa_t_kernel(
 
         def second_matmul(i):
             n_codes, n_scales = live["n_mx", i]
-            kv = psum.tile([P, KVW], F32, tag="kv")
+            kv = psum.tile([P, KVW], F32, tag="short", bufs=SHORT_BANKS)
             nc.tensor.matmul_mx(
                 out=kv[:],
                 lhsT=n_codes[:].bitcast(FP8X4), lhsT_scale=n_scales[:],
@@ -298,7 +299,7 @@ def tile_multiheadlatentattention_pa_t_kernel(
             group_x(i)
             quantise_x(i)
 
-        gain_ps = psum.tile([P, LORA], F32, tag="kv")
+        gain_ps = psum.tile([P, LORA], F32, tag="short", bufs=SHORT_BANKS)
         nc.tensor.matmul(gain_ps[:], lhsT=ones[:], rhs=gain_rows[:], start=True, stop=True)
         nc.scalar.copy(
             out=gain[:].rearrange("p (u m e) -> p u m e", u=2, e=2),

@@ -23,7 +23,6 @@ TILES = B * J
 HALF = ROPE // 2
 X_LEAD = 2
 ROPE_LAG = 1
-LATE_PER_STEP = 2
 SHORT_BANKS = 4
 
 FLOPS = 2 * B * T * C * (LORA + ROPE) + 2 * B * T * LORA * KVW
@@ -281,23 +280,19 @@ def tile_multiheadlatentattention_pa_t_kernel(
             )
 
         lat_pieces = [(lat_raws[g], w_codes[:, g, 0:LORA], w_scales[:, g, 0:LORA]) for g in range(PASSES)]
-        late_pieces = [
+        rope_pieces = [
             (rope_raws[g], w_codes[:, g, LORA : LORA + ROPE], w_scales[:, g, LORA : LORA + ROPE])
             for g in range(PASSES)
         ]
-        late_pieces.append((wd_raw, wd_codes[:], wd_scales[:]))
+        wd_piece = (wd_raw, wd_codes[:], wd_scales[:])
 
         transpose_x(0)
-        group_x(0)
         grouped_0 = regroup_piece(lat_pieces[0], regroup_permuted)
-        quantise_x(0)
+        group_x(0)
         grouped_1 = regroup_piece(lat_pieces[1], regroup_permuted)
         quantise_piece(lat_pieces[0], grouped_0)
+        quantise_x(0)
         quantise_piece(lat_pieces[1], grouped_1)
-        for i in range(1, X_LEAD):
-            transpose_x(i)
-            group_x(i)
-            quantise_x(i)
 
         gain_ps = psum.tile([P, LORA], F32, tag="short", bufs=SHORT_BANKS)
         nc.tensor.matmul(gain_ps[:], lhsT=ones[:], rhs=gain_rows[:], start=True, stop=True)
@@ -305,13 +300,17 @@ def tile_multiheadlatentattention_pa_t_kernel(
             out=gain[:].rearrange("p (u m e) -> p u m e", u=2, e=2),
             in_=gain_ps[:].rearrange("p (m u e) -> p u m e", u=2, e=2),
         )
+        for i in range(1, X_LEAD):
+            transpose_x(i)
+            group_x(i)
+            quantise_x(i)
 
         def run(stage_fn, i):
             if 0 <= i < TILES:
                 stage_fn(i)
 
         for s in range(TILES + 4):
-            late_now = late_pieces[LATE_PER_STEP * s : LATE_PER_STEP * (s + 1)]
+            late_now = rope_pieces if s == 0 else []
             run(transpose_x, s + X_LEAD)
             run(transpose_n, s - 2)
             run(copy_kv, s - 4)
@@ -330,4 +329,8 @@ def tile_multiheadlatentattention_pa_t_kernel(
             run(quantise_n, s - 2)
             for piece, w_grouped in zip(late_now, late_grouped):
                 quantise_piece(piece, w_grouped)
+            if s == 1:
+                live["wd_grouped"] = regroup_piece(wd_piece)
+            if s == 2:
+                quantise_piece(wd_piece, live["wd_grouped"])
             run(rotate_sum, s - ROPE_LAG - 1)

@@ -112,10 +112,10 @@ def tile_multiheadlatentattention_pa_t_kernel(
         nc.sync.dma_start(out=table[:, J // 2 : J, :], in_=table_view[:, J // 2 : J, :])
         load_x(TILES - len(x_tiles))
 
-        w_codes = keep.tile([P, PASSES, LORA + ROPE], U32, align_bytes=64)
-        w_scales = keep.tile([P, PASSES, LORA + ROPE], U8, align_bytes=64)
-        wd_codes = keep.tile([P, KVW], U32, align_bytes=64)
-        wd_scales = keep.tile([P, KVW], U8, align_bytes=64)
+        w_codes = keep.tile([P, PASSES, LORA + ROPE], U32, align_bytes=256)
+        w_scales = keep.tile([P, PASSES, LORA + ROPE], U8, align_bytes=256)
+        wd_codes = keep.tile([P, KVW], U32, align_bytes=256)
+        wd_scales = keep.tile([P, KVW], U8, align_bytes=256)
         gain = keep.tile([P, LORA], F32)
 
         live = {}
@@ -140,8 +140,8 @@ def tile_multiheadlatentattention_pa_t_kernel(
 
         def quantise_x(i):
             x_grouped = live["x_grouped", i]
-            x_codes = work.tile([P, PASSES * P], U32, bufs=X_LEAD + ROPE_LAG + 1, align_bytes=64)
-            x_scales = work.tile([P, PASSES * P], U8, bufs=X_LEAD + ROPE_LAG + 1, align_bytes=64)
+            x_codes = work.tile([P, PASSES * P], U32, bufs=X_LEAD + ROPE_LAG + 1, align_bytes=256)
+            x_scales = work.tile([P, PASSES * P], U8, bufs=X_LEAD + ROPE_LAG + 1, align_bytes=256)
             nc.vector.quantize_mx(out=x_codes[:].bitcast(FP8X4), scales=x_scales[:], in_=x_grouped[:])
             live["x_mx", i] = (x_codes, x_scales)
 
@@ -243,8 +243,8 @@ def tile_multiheadlatentattention_pa_t_kernel(
 
         def quantise_n(i):
             n_grouped = live["n_grouped", i]
-            n_codes = work.tile([P, P], U32, align_bytes=64)
-            n_scales = work.tile([P, P], U8, align_bytes=64)
+            n_codes = work.tile([P, P], U32, align_bytes=256)
+            n_scales = work.tile([P, P], U8, align_bytes=256)
             nc.vector.quantize_mx(
                 out=n_codes[:].bitcast(FP8X4), scales=n_scales[:],
                 in_=n_grouped[:].rearrange("p r t -> p (r t)"),

from contextlib import ExitStack

import concourse.mybir as mybir
from concourse.masks import make_identity

F32 = mybir.dt.float32
BF16 = mybir.dt.bfloat16
U32 = mybir.dt.uint32
U8 = mybir.dt.uint8
FP8X4 = mybir.dt.float8_e4m3fn_x4
ALU = mybir.AluOpType
ACT = mybir.ActivationFunctionType

B, T, C, LORA, ROPE, KVW = 4, 1024, 1024, 512, 512, 512
EPS = 1e-6
P = 128
PACK = 4
K_PASS = P * PACK
PASSES = C // K_PASS
assert PASSES == 2
J = T // P
TILES = B * J
HALF = ROPE // 2
X_LEAD = 2
ROPE_LAG = 1
SHORT_BANKS = 4

FLOPS = 2 * B * T * C * (LORA + ROPE) + 2 * B * T * LORA * KVW


def regroup(nc, grouped, raw, cols):
    split = cols * 3 // 4
    for copy, lo, hi in ((nc.vector.tensor_copy, 0, split), (nc.scalar.copy, split, cols)):
        copy(
            out=grouped[:, lo:hi, :].rearrange("p (c i) t -> p c t i", i=4),
            in_=raw[:, :, lo:hi].rearrange("p t (c i) -> p c t i", i=4),
        )


def regroup_permuted(nc, grouped, raw, cols):
    split = cols // PACK * 3 // 4
    for u in range(2):
        for copy, lo, hi in ((nc.vector.tensor_copy, 0, split), (nc.scalar.copy, split, cols // PACK)):
            copy(
                out=grouped[:].rearrange("p (u m e) t -> p u m e t", u=2, e=2)[:, u, lo:hi, :, :],
                in_=raw[:].rearrange("p t (m u e) -> p u m e t", u=2, e=2)[:, u, lo:hi, :, :],
            )


def tile_multiheadlatentattention_pa_t_kernel(
    tc, x, freq_cis, Wckv, kv_norm_w, Wdkv, out_0, out_1
):
    nc = tc.nc
    x_view = x.rearrange("b (p j) c -> b p j c", j=J)
    table_view = freq_cis.rearrange("(p j) i two -> p j (i two)", j=J)
    kv_view = out_0.rearrange("b (p j) f -> b p j f", j=J)
    rope_view = out_1.rearrange("b (p j) f -> b p j f", j=J)

    with ExitStack() as ctx:
        keep = ctx.enter_context(tc.tile_pool(name="keep", bufs=1))
        x_pool = ctx.enter_context(tc.tile_pool(name="x_pool", bufs=TILES))
        stage = ctx.enter_context(tc.tile_pool(name="stage", bufs=2))
        work = ctx.enter_context(tc.tile_pool(name="work", bufs=3))
        small = ctx.enter_context(tc.tile_pool(name="small", bufs=4))
        outs = ctx.enter_context(tc.tile_pool(name="outs", bufs=6))
        psum = ctx.enter_context(tc.psum_pool(name="psum", bufs=1))
        ctx.enter_context(tc.manual_schedule())

        eps = keep.tile([P, 1], F32)
        nc.vector.memset(eps[:], EPS)
        warm = keep.tile([P, 1], F32)
        nc.scalar.activation(out=warm[:], in_=eps[:], func=ACT.Abs_reciprocal_sqrt)
        ident_f32 = keep.tile([P, P], F32)
        make_identity(nc, ident_f32[:])
        ones = keep.tile([P, P], BF16)
        nc.vector.memset(ones[:], 1.0)
        gain_rows = keep.tile([P, LORA], BF16)
        nc.vector.memset(gain_rows[:], 0.0)

        x_tiles = []

        def load_x(count):
            for i in range(len(x_tiles), len(x_tiles) + count):
                b, j = divmod(i, J)
                x_sb = x_pool.tile([P, C], BF16, name="x_sb")
                nc.sync.dma_start(out=x_sb[:], in_=x_view[b, :, j, :])
                x_tiles.append(x_sb)

        def load_w_half(n0):
            raws = []
            for g in range(PASSES):
                w_raw = stage.tile([P, PACK, LORA], BF16, name="w_raw", bufs=2 * PASSES + 1)
                k0 = K_PASS * g
                nc.sync.dma_start(
                    out=w_raw[:],
                    in_=Wckv[k0 : k0 + K_PASS, n0 : n0 + LORA].rearrange("(p t) c -> p t c", t=PACK),
                )
                raws.append(w_raw)
            return raws

        table = keep.tile([P, J, ROPE], BF16)
        load_x(1)
        lat_raws = load_w_half(0)
        nc.sync.dma_start(out=gain_rows[0:1, :], in_=kv_norm_w.unsqueeze(0))
        load_x(2)
        rope_raws = load_w_half(LORA)
        load_x(1)
        wd_raw = stage.tile([P, PACK, KVW], BF16, name="w_raw", bufs=2 * PASSES + 1)
        nc.sync.dma_start(out=wd_raw[:], in_=Wdkv.rearrange("(p t) n -> p t n", t=PACK))
        nc.sync.dma_start(out=table[:, 0 : J // 2, :], in_=table_view[:, 0 : J // 2, :])
        load_x(2)
        nc.sync.dma_start(out=table[:, J // 2 : J, :], in_=table_view[:, J // 2 : J, :])
        load_x(TILES - len(x_tiles))

        w_codes = keep.tile([P, PASSES, LORA + ROPE], U32, align_bytes=256)
        w_scales = keep.tile([P, PASSES, LORA + ROPE], U8, align_bytes=256)
        wd_codes = keep.tile([P, KVW], U32, align_bytes=256)
        wd_scales = keep.tile([P, KVW], U8, align_bytes=256)
        gain = keep.tile([P, LORA], F32)

        live = {}

        def transpose_x(i):
            words = x_tiles[i][:].bitcast(F32)
            xt = psum.tile([P, PASSES, 2, P], F32, tag="short", bufs=SHORT_BANKS)
            for g in range(PASSES):
                for u in range(2):
                    w0 = 2 * P * g
                    nc.tensor.transpose(xt[:, g, u, :], words[:, w0 + u : w0 + 2 * P : 2], ident_f32[:])
            live["xt", i] = xt

        def group_x(i):
            xt = live["xt", i]
            x_grouped = work.tile([P, PASSES * P * PACK], BF16, align_bytes=64)
            nc.scalar.copy(
                out=x_grouped[:].bitcast(F32).rearrange("p (g r u) -> p g r u", g=PASSES, u=2),
                in_=xt[:].rearrange("p g u r -> p g r u"),
            )
            live["x_grouped", i] = x_grouped

        def quantise_x(i):
            x_grouped = live["x_grouped", i]
            x_codes = work.tile([P, PASSES * P], U32, bufs=X_LEAD + ROPE_LAG + 1, align_bytes=256)
            x_scales = work.tile([P, PASSES * P], U8, bufs=X_LEAD + ROPE_LAG + 1, align_bytes=256)
            nc.vector.quantize_mx(out=x_codes[:].bitcast(FP8X4), scales=x_scales[:], in_=x_grouped[:])
            live["x_mx", i] = (x_codes, x_scales)

        def first_matmul(i, acc, n0):
            x_codes, x_scales = live["x_mx", i]
            for g in range(PASSES):
                tokens = slice(g * P, (g + 1) * P)
                nc.tensor.matmul_mx(
                    out=acc[:],
                    lhsT=x_codes[:, tokens].bitcast(FP8X4),
                    lhsT_scale=x_scales[:, tokens],
                    rhs=w_codes[:, g, n0 : n0 + LORA].bitcast(FP8X4),
                    rhs_scale=w_scales[:, g, n0 : n0 + LORA],
                    start=(g == 0),
                    stop=(g == PASSES - 1),
                )

        def matmul_lat(i):
            lat = psum.tile([P, LORA], F32, tag="lat", bufs=2)
            first_matmul(i, lat, 0)
            live["lat", i] = lat

        def matmul_kr(i):
            kr = psum.tile([P, ROPE], F32, tag="kr", bufs=2)
            first_matmul(i, kr, LORA)
            live["kr", i] = kr

        def sum_squares(i):
            lat = live["lat", i]
            squares = work.tile([P, LORA], BF16)
            sum_sq = small.tile([P, 1], F32)
            nc.scalar.activation(out=squares[:], in_=lat[:], func=ACT.Square, accum_out=sum_sq[:])
            live["sum_sq", i] = sum_sq

        def invert_rms(i):
            inv_rms = small.tile([P, 1], F32)
            nc.scalar.activation(
                out=inv_rms[:], in_=live["sum_sq", i][:], func=ACT.Abs_reciprocal_sqrt, bias=EPS, scale=1.0 / LORA
            )
            live["inv_rms", i] = inv_rms

        def pairs_of(i):
            kr = live["kr", i][:].rearrange("p (i e) -> p i e", e=2)
            cos_sin = table[:, i % J, :].rearrange("p (i two) -> p i two", two=2)
            return kr, cos_sin

        def rotate_by_cos(i):
            kr, cos_sin = pairs_of(i)
            by_cos = work.tile([P, HALF, 2], F32)
            nc.vector.tensor_tensor(
                out=by_cos[:], in0=kr, in1=cos_sin[:, :, 0:1].to_broadcast([P, HALF, 2]), op=ALU.mult
            )
            live["by_cos", i] = by_cos

        def rotate_by_sin(i):
            kr, cos_sin = pairs_of(i)
            by_sin = work.tile([P, 2, HALF], F32)
            nc.vector.scalar_tensor_tensor(
                out=by_sin[:, 0, :], in0=kr[:, :, 1], scalar=-1.0, in1=cos_sin[:, :, 1],
                op0=ALU.mult, op1=ALU.mult,
            )
            nc.vector.tensor_tensor(out=by_sin[:, 1, :], in0=kr[:, :, 0], in1=cos_sin[:, :, 1], op=ALU.mult)
            live["by_sin", i] = by_sin

        def normalise(i):
            lat = live["lat", i]
            inv_rms = live["inv_rms", i]
            n_bf16 = work.tile([P, LORA], BF16)
            nc.vector.scalar_tensor_tensor(
                out=n_bf16[:], in0=lat[:], scalar=inv_rms[:], in1=gain[:], op0=ALU.mult, op1=ALU.mult
            )
            live["n", i] = n_bf16

        def rotate_sum(i):
            rope_sb = outs.tile([P, ROPE], F32)
            nc.gpsimd.tensor_tensor(
                out=rope_sb[:].rearrange("p (i e) -> p i e", e=2),
                in0=live["by_cos", i][:],
                in1=live["by_sin", i][:].rearrange("p e i -> p i e"),
                op=ALU.add,
            )
            nc.sync.dma_start(out=rope_view[i // J, :, i % J, :], in_=rope_sb[:])

        def transpose_n(i):
            words = live["n", i][:].bitcast(F32)
            nt = psum.tile([P, 2, P], F32, tag="short", bufs=SHORT_BANKS)
            for u in range(2):
                nc.tensor.transpose(nt[:, u, :], words[:, u * P : (u + 1) * P], ident_f32[:])
            live["nt", i] = nt

        def group_n(i):
            nt = live["nt", i]
            n_grouped = work.tile([P, P, PACK], BF16, align_bytes=64)
            nc.scalar.copy(
                out=n_grouped[:].rearrange("p r t -> p (r t)").bitcast(F32).rearrange("p (r u) -> p r u", u=2),
                in_=nt[:].rearrange("p u r -> p r u"),
            )
            live["n_grouped", i] = n_grouped

        def quantise_n(i):
            n_grouped = live["n_grouped", i]
            n_codes = work.tile([P, P], U32, align_bytes=256)
            n_scales = work.tile([P, P], U8, align_bytes=256)
            nc.vector.quantize_mx(
                out=n_codes[:].bitcast(FP8X4), scales=n_scales[:],
                in_=n_grouped[:].rearrange("p r t -> p (r t)"),
            )
            live["n_mx", i] = (n_codes, n_scales)

        def second_matmul(i):
            n_codes, n_scales = live["n_mx", i]
            kv = psum.tile([P, KVW], F32, tag="short", bufs=SHORT_BANKS)
            nc.tensor.matmul_mx(
                out=kv[:],
                lhsT=n_codes[:].bitcast(FP8X4), lhsT_scale=n_scales[:],
                rhs=wd_codes[:].bitcast(FP8X4), rhs_scale=wd_scales[:],
                start=True, stop=True,
            )
            live["kv", i] = kv

        def copy_kv(i):
            kv_sb = outs.tile([P, KVW], F32)
            nc.scalar.copy(out=kv_sb[:], in_=live["kv", i][:])
            nc.sync.dma_start(out=kv_view[i // J, :, i % J, :], in_=kv_sb[:])

        def regroup_piece(piece, regroup_fn=regroup):
            w_grouped = stage.tile([P, LORA, PACK], BF16, bufs=3, align_bytes=64)
            regroup_fn(nc, w_grouped, piece[0], LORA)
            return w_grouped

        def quantise_piece(piece, w_grouped):
            nc.vector.quantize_mx(
                out=piece[1].bitcast(FP8X4),
                scales=piece[2],
                in_=w_grouped[:].rearrange("p c t -> p (c t)"),
            )

        lat_pieces = [(lat_raws[g], w_codes[:, g, 0:LORA], w_scales[:, g, 0:LORA]) for g in range(PASSES)]
        rope_pieces = [
            (rope_raws[g], w_codes[:, g, LORA : LORA + ROPE], w_scales[:, g, LORA : LORA + ROPE])
            for g in range(PASSES)
        ]
        wd_piece = (wd_raw, wd_codes[:], wd_scales[:])

        transpose_x(0)
        grouped_0 = regroup_piece(lat_pieces[0], regroup_permuted)
        group_x(0)
        grouped_1 = regroup_piece(lat_pieces[1], regroup_permuted)
        quantise_piece(lat_pieces[0], grouped_0)
        quantise_x(0)
        quantise_piece(lat_pieces[1], grouped_1)

        gain_ps = psum.tile([P, LORA], F32, tag="short", bufs=SHORT_BANKS)
        nc.tensor.matmul(gain_ps[:], lhsT=ones[:], rhs=gain_rows[:], start=True, stop=True)
        nc.scalar.copy(
            out=gain[:].rearrange("p (u m e) -> p u m e", u=2, e=2),
            in_=gain_ps[:].rearrange("p (m u e) -> p u m e", u=2, e=2),
        )
        for i in range(1, X_LEAD):
            transpose_x(i)
            group_x(i)
            quantise_x(i)

        def run(stage_fn, i):
            if 0 <= i < TILES:
                stage_fn(i)

        for s in range(TILES + 4):
            late_now = rope_pieces if s == 0 else []
            run(transpose_x, s + X_LEAD)
            run(transpose_n, s - 2)
            run(copy_kv, s - 4)
            run(group_x, s + X_LEAD)
            run(group_n, s - 2)
            late_grouped = [regroup_piece(piece) for piece in late_now]
            run(matmul_lat, s)
            run(matmul_kr, s - ROPE_LAG)
            run(second_matmul, s - 3)
            run(sum_squares, s)
            run(invert_rms, s)
            run(rotate_by_cos, s - ROPE_LAG - 1)
            run(normalise, s - 1)
            run(rotate_by_sin, s - ROPE_LAG - 1)
            run(quantise_x, s + X_LEAD)
            run(quantise_n, s - 2)
            for piece, w_grouped in zip(late_now, late_grouped):
                quantise_piece(piece, w_grouped)
            if s == 1:
                live["wd_grouped"] = regroup_piece(wd_piece)
            if s == 2:
                quantise_piece(wd_piece, live["wd_grouped"])
            run(rotate_sum, s - ROPE_LAG - 1)
